import numpy as np
import ml_dtypes


def mxq(x, axis, fmt="e4m3"):
    dtype, down = {"e4m3": (ml_dtypes.float8_e4m3fn, 7), "e5m2": (ml_dtypes.float8_e5m2, 14)}[fmt]
    v = np.moveaxis(np.asarray(x, np.float32).astype(ml_dtypes.bfloat16).astype(np.float64), axis, -1)
    blocks = v.reshape(v.shape[:-1] + (-1, 32))
    amax = np.abs(blocks).max(-1, keepdims=True)
    byte = np.maximum(np.where(amax > 0, np.frexp(amax)[1] - 1 + 127, 0) - down, 1)
    scale = np.exp2(byte - 127.0)
    codes = (blocks / scale).astype(np.float32).astype(dtype).astype(np.float64)
    return np.moveaxis((codes * scale).reshape(v.shape), -1, axis)


WIDE = False


def mx_kscale(k):
    if not WIDE:
        return np.ones(k)
    levels = np.array([10, -10, 5, -5, 0])
    if k % 512:
        return np.exp2(np.random.permutation(np.resize(levels, k // 32))).repeat(32)
    a = np.empty((k // 512, 16))
    for p in range(k // 512):
        a[p, :8] = np.random.permutation(np.resize(levels, 8))
        for g in range(8):
            far = levels[np.abs(levels - a[p, g]) >= 10]
            a[p, g + 8] = far[np.random.randint(len(far))]
    return np.exp2(a.ravel()).repeat(32)


BF16 = ml_dtypes.bfloat16


def bf(x):
    return np.asarray(x, np.float32).astype(BF16)


def f64(x):
    return np.asarray(x).astype(np.float64)


M, N0, N1, N2, N3, R0, R1, R2, R3, R4 = 8192, 128, 8, 1, 128, 1, 128, 512, 128, 1
IN = N0 * N1
OUT = N2 * N3 * R4


def setup_inputs():
    s = mx_kscale(IN)
    return {"x": bf(np.random.standard_normal((M, IN)) * s),
            "tt_prefix": bf(np.random.standard_normal((IN * N2, R3)) / np.repeat(s, N2)[:, None]),
            "core3": bf(np.random.standard_normal((R3, N3, R4)) / np.sqrt(R3 * IN))}


def reference(x, tt_prefix, core3):
    w = (f64(tt_prefix) @ f64(core3).reshape(R3, N3 * R4)).reshape(IN, OUT)
    return mxq(f64(x), 1, "e4m3") @ mxq(w, 0, "e4m3")

@@ -1,0 +1,189 @@
+import concourse.mybir as mybir
+from concourse.masks import make_identity
+
+F32 = mybir.dt.float32
+BF16 = mybir.dt.bfloat16
+U32 = mybir.dt.uint32
+U8 = mybir.dt.uint8
+FP8X4 = mybir.dt.float8_e4m3fn_x4
+
+P = 128
+ROWS = 8192
+K = 1024
+N = 128
+RANK = 128
+TILES = ROWS // P
+WORDS = K // 2
+QUAD = 4
+STEPS = TILES // QUAD
+XT_BANKS = 6
+LOADS = [2, 2] + [4] * 14 + [2, 2]
+STORES = [8, 4, 2, 1, 1]
+
+FLOPS = 2 * ROWS * K * N + 2 * K * RANK * N
+
+
+def tile_tttlayer_pb_t_kernel(tc, x, tt_prefix, core3, out):
+    nc = tc.nc
+    x_view = x.rearrange("(p t) k -> p t k", t=TILES)
+    out_view = out.rearrange("(p t) n -> p t n", t=TILES)
+
+    with tc.tile_pool(name="const", bufs=1) as const, tc.tile_pool(
+        name="xin", bufs=1
+    ) as xin, tc.tile_pool(name="work", bufs=1) as work, tc.tile_pool(
+        name="res", bufs=1
+    ) as res, tc.psum_pool(name="psum", bufs=1) as psum, tc.manual_schedule():
+        core_sb = const.tile([P, N], BF16, name="core_sb")
+        nc.sync.dma_start(out=core_sb[:], in_=core3.rearrange("c n o -> c (n o)"))
+        tt_sb = const.tile([P, 2, 4, RANK], BF16, name="tt_sb")
+        nc.sync.dma_start(
+            out=tt_sb[:], in_=tt_prefix.rearrange("(g p t) c -> p g t c", g=2, t=4)
+        )
+        x_of = []
+        first = 0
+        for i, count in enumerate(LOADS):
+            x_sb = xin.tile([P, count, K], BF16, name="x%d" % i)
+            nc.sync.dma_start(out=x_sb[:], in_=x_view[:, first : first + count, :])
+            for j in range(count):
+                x_of.append((x_sb, j))
+            first += count
+
+        ident_bf = const.tile([P, P], BF16, name="ident_bf")
+        make_identity(nc, ident_bf[:])
+        ident = const.tile([P, P], F32, name="ident")
+        make_identity(nc, ident[:])
+
+        w_grouped = const.tile([P, 2, N, 4], BF16, name="w_grouped", align_bytes=64)
+        w_codes = const.tile([P, 2 * N], U32, name="w_codes", align_bytes=64)
+        w_scales = const.tile([P, 2 * N], U8, name="w_scales", align_bytes=64)
+        ttT_sb = const.tile([P, 8, P], BF16, name="ttT_sb")
+
+        grouped = {}
+        codes = {}
+        scales = {}
+        acc = {}
+        xt = {}
+        out_of = {}
+        store_at = {}
+        first = 0
+        for i, count in enumerate(STORES):
+            out_sb = res.tile([P, count * QUAD, N], F32, name="out%d" % i)
+            for j in range(count):
+                out_of[first + j] = (out_sb, j)
+            store_at[first + count - 1] = (out_sb, first, count)
+            first += count
+
+        def weight_transposes():
+            ttT_ps = psum.tile([P, 8, P], BF16, name="ttT_ps", tag="acc0")
+            for j in range(8):
+                nc.tensor.transpose(
+                    ttT_ps[:, j, :],
+                    tt_sb[:, j // 4, j % 4, :],
+                    ident_bf[:],
+                )
+            nc.vector.tensor_copy(out=ttT_sb[:], in_=ttT_ps[:])
+
+        def weight_product():
+            for g in range(2):
+                w_ps = psum.tile([P, 4, N], F32, name="w_ps%d" % g, tag="acc%d" % (1 - g))
+                for t in range(4):
+                    nc.tensor.matmul(
+                        w_ps[:, t, :],
+                        lhsT=ttT_sb[:, 4 * g + t, :],
+                        rhs=core_sb[:],
+                        start=True,
+                        stop=True,
+                    )
+                nc.vector.tensor_copy(
+                    out=w_grouped[:, g, :, :], in_=w_ps[:].rearrange("p t n -> p n t")
+                )
+            nc.vector.quantize_mx(
+                out=w_codes[:].bitcast(FP8X4),
+                scales=w_scales[:],
+                in_=w_grouped[:].rearrange("p g n t -> p (g n t)"),
+            )
+
+        def transposes(s):
+            grouped[s] = work.tile(
+                [P, QUAD * K], BF16, name="grouped%d" % s, tag="grouped%d" % (s % 3), align_bytes=64
+            )
+            for q in range(QUAD):
+                t = QUAD * s + q
+                x_sb, j = x_of[t]
+                words = x_sb[:, j, :].bitcast(F32)
+                xt[t] = psum.tile([P, 4, P], F32, name="xt%d" % t, tag="xt%d" % (t % XT_BANKS))
+                for b in range(4):
+                    first_word = 2 * P * (b // 2) + b % 2
+                    nc.tensor.transpose(
+                        xt[t][:, b, :], words[:, first_word : 2 * P * (b // 2 + 1) : 2], ident[:]
+                    )
+
+        def copies(s):
+            dst = grouped[s][:].bitcast(F32)
+            for q in range(QUAD):
+                t = QUAD * s + q
+                d = dst[:, q * WORDS : (q + 1) * WORDS].rearrange(
+                    "p (g r u) -> p g r u", g=2, u=2
+                )
+                src = xt[t][:].rearrange("p (g u) r -> p g r u", u=2)
+                if q == QUAD - 1:
+                    nc.vector.tensor_copy(out=d, in_=src)
+                else:
+                    nc.scalar.copy(out=d, in_=src)
+
+        def quantise(s):
+            codes[s] = work.tile(
+                [P, QUAD * K // 4], U32, name="codes%d" % s, tag="codes%d" % (s % 3), align_bytes=64
+            )
+            scales[s] = work.tile(
+                [P, QUAD * K // 4], U8, name="scales%d" % s, tag="scales%d" % (s % 3), align_bytes=64
+            )
+            half = QUAD * K // 2
+            for h in range(2):
+                nc.vector.quantize_mx(
+                    out=codes[s][:, h * half // 4 : (h + 1) * half // 4].bitcast(FP8X4),
+                    scales=scales[s][:, h * half // 4 : (h + 1) * half // 4],
+                    in_=grouped[s][:, h * half : (h + 1) * half],
+                )
+
+        def products(s):
+            acc[s] = psum.tile([P, QUAD, N], F32, name="acc%d" % s, tag="acc%d" % (s % 2))
+            for q in range(QUAD):
+                for g in range(2):
+                    c0 = (2 * q + g) * P
+                    nc.tensor.matmul_mx(
+                        out=acc[s][:, q, :],
+                        lhsT=codes[s][:, c0 : c0 + P].bitcast(FP8X4),
+                        lhsT_scale=scales[s][:, c0 : c0 + P],
+                        rhs=w_codes[:, g * N : (g + 1) * N].bitcast(FP8X4),
+                        rhs_scale=w_scales[:, g * N : (g + 1) * N],
+                        start=(g == 0),
+                        stop=(g == 1),
+                    )
+
+        def results(s):
+            out_sb, j = out_of[s]
+            if s % 2 == 1:
+                nc.scalar.copy(out=out_sb[:, j * QUAD : (j + 1) * QUAD, :], in_=acc[s][:])
+            else:
+                nc.vector.tensor_copy(out=out_sb[:, j * QUAD : (j + 1) * QUAD, :], in_=acc[s][:])
+            if s in store_at:
+                tile_sb, first_step, count = store_at[s]
+                nc.sync.dma_start(
+                    out=out_view[:, first_step * QUAD : (first_step + count) * QUAD, :],
+                    in_=tile_sb[:],
+                )
+
+        weight_transposes()
+        for s in range(STEPS + 3):
+            if 0 <= s - 3 < STEPS:
+                results(s - 3)
+            if 0 <= s - 1 < STEPS:
+                quantise(s - 1)
+            if s < STEPS:
+                transposes(s)
+                copies(s)
+            if s == 0:
+                weight_product()
+            if 0 <= s - 2 < STEPS:
+                products(s - 2)

@@ -17,10 +17,21 @@ WORDS = K // 2
 QUAD = 4
 STEPS = TILES // QUAD
 XT_BANKS = 6
-LOADS = [2, 2] + [4] * 14 + [2, 2]
+FIRST_LOADS = [1, 1, 2]
+LOADS = FIRST_LOADS + [4] * 15
 STORES = [8, 4, 2, 1, 1]
+SORT_FROM = 8
+SORTED = 3
 
 FLOPS = 2 * ROWS * K * N + 2 * K * RANK * N
+
+
+def is_sorted(t):
+    return t >= SORT_FROM and t % QUAD >= QUAD - SORTED
+
+
+def vector_copies(t):
+    return t % 8 == 7 or (t < SORT_FROM and t % 4 == 3)
 
 
 def tile_tttlayer_pb_t_kernel(tc, x, tt_prefix, core3, out):
@@ -34,35 +45,36 @@ def tile_tttlayer_pb_t_kernel(tc, x, tt_prefix, core3, out):
         name="res", bufs=1
     ) as res, tc.psum_pool(name="psum", bufs=1) as psum, tc.manual_schedule():
         core_sb = const.tile([P, N], BF16, name="core_sb")
-        nc.sync.dma_start(out=core_sb[:], in_=core3.rearrange("c n o -> c (n o)"))
         tt_sb = const.tile([P, 2, 4, RANK], BF16, name="tt_sb")
-        nc.sync.dma_start(
-            out=tt_sb[:], in_=tt_prefix.rearrange("(g p t) c -> p g t c", g=2, t=4)
-        )
         x_of = []
         first = 0
         for i, count in enumerate(LOADS):
+            if i == len(FIRST_LOADS):
+                nc.sync.dma_start(out=tt_sb[:], in_=tt_prefix.rearrange("(g p t) c -> p g t c", g=2, t=4))
+                nc.sync.dma_start(out=core_sb[:], in_=core3.rearrange("c n o -> c (n o)"))
             x_sb = xin.tile([P, count, K], BF16, name="x%d" % i)
             nc.sync.dma_start(out=x_sb[:], in_=x_view[:, first : first + count, :])
             for j in range(count):
                 x_of.append((x_sb, j))
             first += count
 
-        ident_bf = const.tile([P, P], BF16, name="ident_bf")
-        make_identity(nc, ident_bf[:])
         ident = const.tile([P, P], F32, name="ident")
         make_identity(nc, ident[:])
+        ident_bf = const.tile([P, P], BF16, name="ident_bf")
+        make_identity(nc, ident_bf[:])
 
         w_grouped = const.tile([P, 2, N, 4], BF16, name="w_grouped", align_bytes=64)
         w_codes = const.tile([P, 2 * N], U32, name="w_codes", align_bytes=64)
         w_scales = const.tile([P, 2 * N], U8, name="w_scales", align_bytes=64)
         ttT_sb = const.tile([P, 8, P], BF16, name="ttT_sb")
 
+        sorted_of = {}
         grouped = {}
         codes = {}
         scales = {}
         acc = {}
         xt = {}
+        w_ps = {}
         out_of = {}
         store_at = {}
         first = 0
@@ -74,28 +86,25 @@ def tile_tttlayer_pb_t_kernel(tc, x, tt_prefix, core3, out):
             first += count
 
         def weight_transposes():
-            ttT_ps = psum.tile([P, 8, P], BF16, name="ttT_ps", tag="acc0")
+            w_ps["ttT"] = psum.tile([P, 8, P], BF16, name="ttT_ps", tag="acc0")
             for j in range(8):
-                nc.tensor.transpose(
-                    ttT_ps[:, j, :],
-                    tt_sb[:, j // 4, j % 4, :],
-                    ident_bf[:],
-                )
-            nc.vector.tensor_copy(out=ttT_sb[:], in_=ttT_ps[:])
+                nc.tensor.transpose(w_ps["ttT"][:, j, :], tt_sb[:, j // 4, j % 4, :], ident_bf[:])
 
-        def weight_product():
+        def weight_transposes_out():
+            nc.vector.tensor_copy(out=ttT_sb[:], in_=w_ps["ttT"][:])
+
+        def weight_products():
             for g in range(2):
-                w_ps = psum.tile([P, 4, N], F32, name="w_ps%d" % g, tag="acc%d" % (1 - g))
+                w_ps[g] = psum.tile([P, 4, N], F32, name="w_ps%d" % g, tag="acc%d" % (1 - g))
                 for t in range(4):
                     nc.tensor.matmul(
-                        w_ps[:, t, :],
-                        lhsT=ttT_sb[:, 4 * g + t, :],
-                        rhs=core_sb[:],
-                        start=True,
-                        stop=True,
+                        w_ps[g][:, t, :], lhsT=ttT_sb[:, 4 * g + t, :], rhs=core_sb[:], start=True, stop=True
                     )
+
+        def weight_quantise():
+            for g in range(2):
                 nc.vector.tensor_copy(
-                    out=w_grouped[:, g, :, :], in_=w_ps[:].rearrange("p t n -> p n t")
+                    out=w_grouped[:, g, :, :], in_=w_ps[g][:].rearrange("p t n -> p n t")
                 )
             nc.vector.quantize_mx(
                 out=w_codes[:].bitcast(FP8X4),
@@ -103,30 +112,41 @@ def tile_tttlayer_pb_t_kernel(tc, x, tt_prefix, core3, out):
                 in_=w_grouped[:].rearrange("p g n t -> p (g n t)"),
             )
 
+        def sort_words(s):
+            for t in range(QUAD * s, QUAD * (s + 1)):
+                if is_sorted(t):
+                    x_sb, j = x_of[t]
+                    sorted_of[t] = work.tile(
+                        [P, WORDS], F32, name="sorted%d" % t, tag="sorted%d" % (t % (2 * QUAD))
+                    )
+                    nc.vector.tensor_copy(
+                        out=sorted_of[t][:].rearrange("p (g u w) -> p g u w", g=2, u=2),
+                        in_=x_sb[:, j, :].bitcast(F32).rearrange("p (g w u) -> p g u w", g=2, u=2),
+                    )
+
         def transposes(s):
-            grouped[s] = work.tile(
-                [P, QUAD * K], BF16, name="grouped%d" % s, tag="grouped%d" % (s % 3), align_bytes=64
-            )
-            for q in range(QUAD):
-                t = QUAD * s + q
+            for t in range(QUAD * s, QUAD * (s + 1)):
                 x_sb, j = x_of[t]
                 words = x_sb[:, j, :].bitcast(F32)
                 xt[t] = psum.tile([P, 4, P], F32, name="xt%d" % t, tag="xt%d" % (t % XT_BANKS))
                 for b in range(4):
-                    first_word = 2 * P * (b // 2) + b % 2
-                    nc.tensor.transpose(
-                        xt[t][:, b, :], words[:, first_word : 2 * P * (b // 2 + 1) : 2], ident[:]
-                    )
+                    if t in sorted_of:
+                        part = sorted_of[t][:, b * P : (b + 1) * P]
+                    else:
+                        first_word = 2 * P * (b // 2) + b % 2
+                        part = words[:, first_word : 2 * P * (b // 2 + 1) : 2]
+                    nc.tensor.transpose(xt[t][:, b, :], part, ident[:])
 
         def copies(s):
+            grouped[s] = work.tile(
+                [P, QUAD * K], BF16, name="grouped%d" % s, tag="grouped%d" % (s % 3), align_bytes=64
+            )
             dst = grouped[s][:].bitcast(F32)
             for q in range(QUAD):
                 t = QUAD * s + q
-                d = dst[:, q * WORDS : (q + 1) * WORDS].rearrange(
-                    "p (g r u) -> p g r u", g=2, u=2
-                )
+                d = dst[:, q * WORDS : (q + 1) * WORDS].rearrange("p (g r u) -> p g r u", g=2, u=2)
                 src = xt[t][:].rearrange("p (g u) r -> p g r u", u=2)
-                if q == QUAD - 1:
+                if vector_copies(t):
                     nc.vector.tensor_copy(out=d, in_=src)
                 else:
                     nc.scalar.copy(out=d, in_=src)
@@ -163,10 +183,7 @@ def tile_tttlayer_pb_t_kernel(tc, x, tt_prefix, core3, out):
 
         def results(s):
             out_sb, j = out_of[s]
-            if s % 2 == 1:
-                nc.scalar.copy(out=out_sb[:, j * QUAD : (j + 1) * QUAD, :], in_=acc[s][:])
-            else:
-                nc.vector.tensor_copy(out=out_sb[:, j * QUAD : (j + 1) * QUAD, :], in_=acc[s][:])
+            nc.scalar.copy(out=out_sb[:, j * QUAD : (j + 1) * QUAD, :], in_=acc[s][:])
             if s in store_at:
                 tile_sb, first_step, count = store_at[s]
                 nc.sync.dma_start(
@@ -174,16 +191,23 @@ def tile_tttlayer_pb_t_kernel(tc, x, tt_prefix, core3, out):
                     in_=tile_sb[:],
                 )
 
-        weight_transposes()
-        for s in range(STEPS + 3):
-            if 0 <= s - 3 < STEPS:
-                results(s - 3)
-            if 0 <= s - 1 < STEPS:
-                quantise(s - 1)
-            if s < STEPS:
-                transposes(s)
-                copies(s)
-            if s == 0:
-                weight_product()
-            if 0 <= s - 2 < STEPS:
-                products(s - 2)
+        for r in range(STEPS + 3):
+            if 0 <= r - 3 < STEPS:
+                results(r - 3)
+            if r == 1:
+                weight_transposes_out()
+            if 0 <= r - 1 < STEPS:
+                quantise(r - 1)
+            if r == 2:
+                weight_quantise()
+            if r + 1 < STEPS:
+                sort_words(r + 1)
+            if r < STEPS:
+                transposes(r)
+                copies(r)
+            if r == 0:
+                weight_transposes()
+            if r == 1:
+                weight_products()
+            if 0 <= r - 2 < STEPS:
+                products(r - 2)

@@ -15,12 +15,14 @@ RANK = 128
 TILES = ROWS // P
 WORDS = K // 2
 QUAD = 4
-STEPS = TILES // QUAD
+STEP_TILES = [2, 2] + [QUAD] * 14 + [2, 2]
+STEPS = len(STEP_TILES)
+PRODUCT_LAG = 3
 XT_BANKS = 6
-FIRST_LOADS = [1, 1, 2]
-LOADS = FIRST_LOADS + [4] * 15
-STORES = [8, 4, 2, 1, 1]
-SORT_FROM = 8
+FIRST_LOADS = [1, 1]
+LOADS = FIRST_LOADS + [2] + [4] * 15
+STORES = [32, 16, 8, 4, 2, 2]
+SORT_FROM = 12
 SORTED = 3
 
 FLOPS = 2 * ROWS * K * N + 2 * K * RANK * N
@@ -31,7 +33,7 @@ def is_sorted(t):
 
 
 def vector_copies(t):
-    return t % 8 == 7 or (t < SORT_FROM and t % 4 == 3)
+    return False
 
 
 def tile_tttlayer_pb_t_kernel(tc, x, tt_prefix, core3, out):
@@ -75,11 +77,16 @@ def tile_tttlayer_pb_t_kernel(tc, x, tt_prefix, core3, out):
         acc = {}
         xt = {}
         w_ps = {}
+        step_tiles = []
+        first = 0
+        for count in STEP_TILES:
+            step_tiles.append(range(first, first + count))
+            first += count
         out_of = {}
         store_at = {}
         first = 0
         for i, count in enumerate(STORES):
-            out_sb = res.tile([P, count * QUAD, N], F32, name="out%d" % i)
+            out_sb = res.tile([P, count, N], F32, name="out%d" % i)
             for j in range(count):
                 out_of[first + j] = (out_sb, j)
             store_at[first + count - 1] = (out_sb, first, count)
@@ -113,7 +120,7 @@ def tile_tttlayer_pb_t_kernel(tc, x, tt_prefix, core3, out):
             )
 
         def sort_words(s):
-            for t in range(QUAD * s, QUAD * (s + 1)):
+            for t in step_tiles[s]:
                 if is_sorted(t):
                     x_sb, j = x_of[t]
                     sorted_of[t] = work.tile(
@@ -125,7 +132,7 @@ def tile_tttlayer_pb_t_kernel(tc, x, tt_prefix, core3, out):
                     )
 
         def transposes(s):
-            for t in range(QUAD * s, QUAD * (s + 1)):
+            for t in step_tiles[s]:
                 x_sb, j = x_of[t]
                 words = x_sb[:, j, :].bitcast(F32)
                 xt[t] = psum.tile([P, 4, P], F32, name="xt%d" % t, tag="xt%d" % (t % XT_BANKS))
@@ -142,8 +149,7 @@ def tile_tttlayer_pb_t_kernel(tc, x, tt_prefix, core3, out):
                 [P, QUAD * K], BF16, name="grouped%d" % s, tag="grouped%d" % (s % 3), align_bytes=64
             )
             dst = grouped[s][:].bitcast(F32)
-            for q in range(QUAD):
-                t = QUAD * s + q
+            for q, t in enumerate(step_tiles[s]):
                 d = dst[:, q * WORDS : (q + 1) * WORDS].rearrange("p (g r u) -> p g r u", g=2, u=2)
                 src = xt[t][:].rearrange("p (g u) r -> p g r u", u=2)
                 if vector_copies(t):
@@ -153,13 +159,13 @@ def tile_tttlayer_pb_t_kernel(tc, x, tt_prefix, core3, out):
 
         def quantise(s):
             codes[s] = work.tile(
-                [P, QUAD * K // 4], U32, name="codes%d" % s, tag="codes%d" % (s % 3), align_bytes=64
+                [P, QUAD * K // 4], U32, name="codes%d" % s, tag="codes%d" % (s % 4), align_bytes=64
             )
             scales[s] = work.tile(
-                [P, QUAD * K // 4], U8, name="scales%d" % s, tag="scales%d" % (s % 3), align_bytes=64
+                [P, QUAD * K // 4], U8, name="scales%d" % s, tag="scales%d" % (s % 4), align_bytes=64
             )
-            half = QUAD * K // 2
-            for h in range(2):
+            half = 2 * K
+            for h in range(len(step_tiles[s]) // 2):
                 nc.vector.quantize_mx(
                     out=codes[s][:, h * half // 4 : (h + 1) * half // 4].bitcast(FP8X4),
                     scales=scales[s][:, h * half // 4 : (h + 1) * half // 4],
@@ -168,7 +174,7 @@ def tile_tttlayer_pb_t_kernel(tc, x, tt_prefix, core3, out):
 
         def products(s):
             acc[s] = psum.tile([P, QUAD, N], F32, name="acc%d" % s, tag="acc%d" % (s % 2))
-            for q in range(QUAD):
+            for q in range(len(step_tiles[s])):
                 for g in range(2):
                     c0 = (2 * q + g) * P
                     nc.tensor.matmul_mx(
@@ -182,26 +188,30 @@ def tile_tttlayer_pb_t_kernel(tc, x, tt_prefix, core3, out):
                     )
 
         def results(s):
-            out_sb, j = out_of[s]
-            nc.scalar.copy(out=out_sb[:, j * QUAD : (j + 1) * QUAD, :], in_=acc[s][:])
-            if s in store_at:
-                tile_sb, first_step, count = store_at[s]
+            count = len(step_tiles[s])
+            out_sb, j = out_of[step_tiles[s][0]]
+            if s % 2 == 1:
+                nc.vector.tensor_copy(out=out_sb[:, j : j + count, :], in_=acc[s][:, 0:count, :])
+            else:
+                nc.scalar.copy(out=out_sb[:, j : j + count, :], in_=acc[s][:, 0:count, :])
+            last = step_tiles[s][-1]
+            if last in store_at:
+                tile_sb, first_tile, stored = store_at[last]
                 nc.sync.dma_start(
-                    out=out_view[:, first_step * QUAD : (first_step + count) * QUAD, :],
-                    in_=tile_sb[:],
+                    out=out_view[:, first_tile : first_tile + stored, :], in_=tile_sb[:]
                 )
 
-        for r in range(STEPS + 3):
-            if 0 <= r - 3 < STEPS:
-                results(r - 3)
+        for r in range(STEPS + PRODUCT_LAG + 1):
+            if 0 <= r - PRODUCT_LAG - 1 < STEPS:
+                results(r - PRODUCT_LAG - 1)
             if r == 1:
                 weight_transposes_out()
+            if r + 1 < STEPS:
+                sort_words(r + 1)
             if 0 <= r - 1 < STEPS:
                 quantise(r - 1)
             if r == 2:
                 weight_quantise()
-            if r + 1 < STEPS:
-                sort_words(r + 1)
             if r < STEPS:
                 transposes(r)
                 copies(r)
@@ -209,5 +219,5 @@ def tile_tttlayer_pb_t_kernel(tc, x, tt_prefix, core3, out):
                 weight_transposes()
             if r == 1:
                 weight_products()
-            if 0 <= r - 2 < STEPS:
-                products(r - 2)
+            if 0 <= r - PRODUCT_LAG < STEPS:
+                products(r - PRODUCT_LAG)

@@ -127,8 +127,8 @@ def tile_tttlayer_pb_t_kernel(tc, x, tt_prefix, core3, out):
                         [P, WORDS], F32, name="sorted%d" % t, tag="sorted%d" % (t % (2 * QUAD))
                     )
                     nc.vector.tensor_copy(
-                        out=sorted_of[t][:].rearrange("p (g u w) -> p g u w", g=2, u=2),
-                        in_=x_sb[:, j, :].bitcast(F32).rearrange("p (g w u) -> p g u w", g=2, u=2),
+                        out=sorted_of[t][:].rearrange("p (u c i) -> p c u i", u=2, i=4),
+                        in_=x_sb[:, j, :].bitcast(F32).rearrange("p (c i u) -> p c u i", u=2, i=4),
                     )
 
         def transposes(s):
@@ -138,7 +138,8 @@ def tile_tttlayer_pb_t_kernel(tc, x, tt_prefix, core3, out):
                 xt[t] = psum.tile([P, 4, P], F32, name="xt%d" % t, tag="xt%d" % (t % XT_BANKS))
                 for b in range(4):
                     if t in sorted_of:
-                        part = sorted_of[t][:, b * P : (b + 1) * P]
+                        place = 2 * (b % 2) + b // 2
+                        part = sorted_of[t][:, place * P : (place + 1) * P]
                     else:
                         first_word = 2 * P * (b // 2) + b % 2
                         part = words[:, first_word : 2 * P * (b // 2 + 1) : 2]

@@ -23,7 +23,7 @@ FIRST_LOADS = [1, 1]
 LOADS = FIRST_LOADS + [2] + [4] * 15
 STORES = [32, 16, 8, 4, 2, 2]
 SORT_FROM = 12
-SORTED = 3
+SORTED = 2
 
 FLOPS = 2 * ROWS * K * N + 2 * K * RANK * N
 
@@ -191,7 +191,7 @@ def tile_tttlayer_pb_t_kernel(tc, x, tt_prefix, core3, out):
         def results(s):
             count = len(step_tiles[s])
             out_sb, j = out_of[step_tiles[s][0]]
-            if s % 2 == 1:
+            if s % 4 != 3:
                 nc.vector.tensor_copy(out=out_sb[:, j : j + count, :], in_=acc[s][:, 0:count, :])
             else:
                 nc.scalar.copy(out=out_sb[:, j : j + count, :], in_=acc[s][:, 0:count, :])
@@ -207,10 +207,10 @@ def tile_tttlayer_pb_t_kernel(tc, x, tt_prefix, core3, out):
                 results(r - PRODUCT_LAG - 1)
             if r == 1:
                 weight_transposes_out()
-            if r + 1 < STEPS:
-                sort_words(r + 1)
             if 0 <= r - 1 < STEPS:
                 quantise(r - 1)
+            if r + 1 < STEPS:
+                sort_words(r + 1)
             if r == 2:
                 weight_quantise()
             if r < STEPS:

@@ -15,7 +15,7 @@ RANK = 128
 TILES = ROWS // P
 WORDS = K // 2
 QUAD = 4
-STEP_TILES = [2, 2] + [QUAD] * 14 + [2, 2]
+STEP_TILES = [2, 2] + [QUAD] * 14 + [2, 1, 1]
 STEPS = len(STEP_TILES)
 PRODUCT_LAG = 3
 XT_BANKS = 6
@@ -23,13 +23,13 @@ FIRST_LOADS = [1, 1]
 LOADS = FIRST_LOADS + [2] + [4] * 15
 STORES = [32, 16, 8, 4, 2, 2]
 SORT_FROM = 12
-SORTED = 2
+SORT_TO = 60
 
 FLOPS = 2 * ROWS * K * N + 2 * K * RANK * N
 
 
 def is_sorted(t):
-    return t >= SORT_FROM and t % QUAD >= QUAD - SORTED
+    return SORT_FROM <= t < SORT_TO and t % 8 in (1, 2, 3, 6, 7)
 
 
 def vector_copies(t):
@@ -165,16 +165,21 @@ def tile_tttlayer_pb_t_kernel(tc, x, tt_prefix, core3, out):
             scales[s] = work.tile(
                 [P, QUAD * K // 4], U8, name="scales%d" % s, tag="scales%d" % (s % 4), align_bytes=64
             )
-            half = 2 * K
-            for h in range(len(step_tiles[s]) // 2):
+            half = K * min(2, len(step_tiles[s]))
+            for h in range((len(step_tiles[s]) + 1) // 2):
                 nc.vector.quantize_mx(
                     out=codes[s][:, h * half // 4 : (h + 1) * half // 4].bitcast(FP8X4),
                     scales=scales[s][:, h * half // 4 : (h + 1) * half // 4],
                     in_=grouped[s][:, h * half : (h + 1) * half],
                 )
 
+        def acc_tag(s):
+            if s >= STEPS - 2:
+                return "xt%d" % ((TILES - 6 + s - (STEPS - 2)) % XT_BANKS)
+            return "acc%d" % (s % 2)
+
         def products(s):
-            acc[s] = psum.tile([P, QUAD, N], F32, name="acc%d" % s, tag="acc%d" % (s % 2))
+            acc[s] = psum.tile([P, QUAD, N], F32, name="acc%d" % s, tag=acc_tag(s))
             for q in range(len(step_tiles[s])):
                 for g in range(2):
                     c0 = (2 * q + g) * P
@@ -191,7 +196,7 @@ def tile_tttlayer_pb_t_kernel(tc, x, tt_prefix, core3, out):
         def results(s):
             count = len(step_tiles[s])
             out_sb, j = out_of[step_tiles[s][0]]
-            if s % 4 != 3:
+            if s % 3 != 2:
                 nc.vector.tensor_copy(out=out_sb[:, j : j + count, :], in_=acc[s][:, 0:count, :])
             else:
                 nc.scalar.copy(out=out_sb[:, j : j + count, :], in_=acc[s][:, 0:count, :])

@@ -20,7 +20,7 @@ STEPS = len(STEP_TILES)
 PRODUCT_LAG = 3
 XT_BANKS = 6
 FIRST_LOADS = [1, 1]
-LOADS = FIRST_LOADS + [2] + [4] * 15
+LOADS = FIRST_LOADS + [2] * 7 + [4] * 12
 STORES = [32, 16, 8, 4, 2, 2]
 SORT_FROM = 12
 SORT_TO = 60
@@ -196,7 +196,7 @@ def tile_tttlayer_pb_t_kernel(tc, x, tt_prefix, core3, out):
         def results(s):
             count = len(step_tiles[s])
             out_sb, j = out_of[step_tiles[s][0]]
-            if s % 3 != 2:
+            if s % 3 != 2 and not STEPS - 5 < s < STEPS - 1:
                 nc.vector.tensor_copy(out=out_sb[:, j : j + count, :], in_=acc[s][:, 0:count, :])
             else:
                 nc.scalar.copy(out=out_sb[:, j : j + count, :], in_=acc[s][:, 0:count, :])

@@ -19,9 +19,9 @@ STEP_TILES = [2, 2] + [QUAD] * 14 + [2, 1, 1]
 STEPS = len(STEP_TILES)
 PRODUCT_LAG = 3
 XT_BANKS = 6
-FIRST_LOADS = [1, 1]
-LOADS = FIRST_LOADS + [2] * 7 + [4] * 12
-STORES = [32, 16, 8, 4, 2, 2]
+FIRST_LOADS = [2]
+LOADS = FIRST_LOADS + [2] + [4] * 15
+STORES = [32, 16, 8, 4, 4]
 SORT_FROM = 12
 SORT_TO = 60
 

@@ -19,6 +19,7 @@ STEP_TILES = [2, 2] + [QUAD] * 14 + [2, 1, 1]
 STEPS = len(STEP_TILES)
 PRODUCT_LAG = 3
 XT_BANKS = 6
+GROUP = 8
 FIRST_LOADS = [2]
 LOADS = FIRST_LOADS + [2] + [4] * 15
 STORES = [32, 16, 8, 4, 4]
@@ -38,8 +39,8 @@ def vector_copies(t):
 
 def tile_tttlayer_pb_t_kernel(tc, x, tt_prefix, core3, out):
     nc = tc.nc
-    x_view = x.rearrange("(p t) k -> p t k", t=TILES)
-    out_view = out.rearrange("(p t) n -> p t n", t=TILES)
+    x_view = x.rearrange("(s p j) k -> s p j k", p=P, j=GROUP)
+    out_view = out.rearrange("(s p j) n -> p s j n", p=P, j=GROUP)
 
     with tc.tile_pool(name="const", bufs=1) as const, tc.tile_pool(
         name="xin", bufs=1
@@ -55,7 +56,8 @@ def tile_tttlayer_pb_t_kernel(tc, x, tt_prefix, core3, out):
                 nc.sync.dma_start(out=tt_sb[:], in_=tt_prefix.rearrange("(g p t) c -> p g t c", g=2, t=4))
                 nc.sync.dma_start(out=core_sb[:], in_=core3.rearrange("c n o -> c (n o)"))
             x_sb = xin.tile([P, count, K], BF16, name="x%d" % i)
-            nc.sync.dma_start(out=x_sb[:], in_=x_view[:, first : first + count, :])
+            part = slice(first % GROUP, first % GROUP + count)
+            nc.sync.dma_start(out=x_sb[:], in_=x_view[first // GROUP, :, part, :])
             for j in range(count):
                 x_of.append((x_sb, j))
             first += count
@@ -203,9 +205,15 @@ def tile_tttlayer_pb_t_kernel(tc, x, tt_prefix, core3, out):
             last = step_tiles[s][-1]
             if last in store_at:
                 tile_sb, first_tile, stored = store_at[last]
-                nc.sync.dma_start(
-                    out=out_view[:, first_tile : first_tile + stored, :], in_=tile_sb[:]
-                )
+                group = first_tile // GROUP
+                if stored < GROUP:
+                    part = slice(first_tile % GROUP, first_tile % GROUP + stored)
+                    nc.sync.dma_start(out=out_view[:, group, part, :], in_=tile_sb[:])
+                else:
+                    nc.sync.dma_start(
+                        out=out_view[:, group : group + stored // GROUP, :, :],
+                        in_=tile_sb[:].rearrange("p (s j) n -> p s j n", j=GROUP),
+                    )
 
         for r in range(STEPS + PRODUCT_LAG + 1):
             if 0 <= r - PRODUCT_LAG - 1 < STEPS:

import concourse.mybir as mybir
from concourse.masks import make_identity

F32 = mybir.dt.float32
BF16 = mybir.dt.bfloat16
U32 = mybir.dt.uint32
U8 = mybir.dt.uint8
FP8X4 = mybir.dt.float8_e4m3fn_x4

P = 128
ROWS = 8192
K = 1024
N = 128
RANK = 128
TILES = ROWS // P
WORDS = K // 2
QUAD = 4
STEP_TILES = [2, 2] + [QUAD] * 14 + [2, 1, 1]
STEPS = len(STEP_TILES)
PRODUCT_LAG = 3
XT_BANKS = 6
GROUP = 8
FIRST_LOADS = [2]
LOADS = FIRST_LOADS + [2] + [4] * 15
STORES = [32, 16, 8, 4, 4]
SORT_FROM = 12
SORT_TO = 60

FLOPS = 2 * ROWS * K * N + 2 * K * RANK * N


def is_sorted(t):
    return SORT_FROM <= t < SORT_TO and t % 8 in (1, 2, 3, 6, 7)


def vector_copies(t):
    return False


def tile_tttlayer_pb_t_kernel(tc, x, tt_prefix, core3, out):
    nc = tc.nc
    x_view = x.rearrange("(s p j) k -> s p j k", p=P, j=GROUP)
    out_view = out.rearrange("(s p j) n -> p s j n", p=P, j=GROUP)

    with tc.tile_pool(name="const", bufs=1) as const, tc.tile_pool(
        name="xin", bufs=1
    ) as xin, tc.tile_pool(name="work", bufs=1) as work, tc.tile_pool(
        name="res", bufs=1
    ) as res, tc.psum_pool(name="psum", bufs=1) as psum, tc.manual_schedule():
        core_sb = const.tile([P, N], BF16, name="core_sb")
        tt_sb = const.tile([P, 2, 4, RANK], BF16, name="tt_sb")
        x_of = []
        first = 0
        for i, count in enumerate(LOADS):
            if i == len(FIRST_LOADS):
                nc.sync.dma_start(out=tt_sb[:], in_=tt_prefix.rearrange("(g p t) c -> p g t c", g=2, t=4))
                nc.sync.dma_start(out=core_sb[:], in_=core3.rearrange("c n o -> c (n o)"))
            x_sb = xin.tile([P, count, K], BF16, name="x%d" % i)
            part = slice(first % GROUP, first % GROUP + count)
            nc.sync.dma_start(out=x_sb[:], in_=x_view[first // GROUP, :, part, :])
            for j in range(count):
                x_of.append((x_sb, j))
            first += count

        ident = const.tile([P, P], F32, name="ident")
        make_identity(nc, ident[:])
        ident_bf = const.tile([P, P], BF16, name="ident_bf")
        make_identity(nc, ident_bf[:])

        w_grouped = const.tile([P, 2, N, 4], BF16, name="w_grouped", align_bytes=64)
        w_codes = const.tile([P, 2 * N], U32, name="w_codes", align_bytes=64)
        w_scales = const.tile([P, 2 * N], U8, name="w_scales", align_bytes=64)
        ttT_sb = const.tile([P, 8, P], BF16, name="ttT_sb")

        sorted_of = {}
        grouped = {}
        codes = {}
        scales = {}
        acc = {}
        xt = {}
        w_ps = {}
        step_tiles = []
        first = 0
        for count in STEP_TILES:
            step_tiles.append(range(first, first + count))
            first += count
        out_of = {}
        store_at = {}
        first = 0
        for i, count in enumerate(STORES):
            out_sb = res.tile([P, count, N], F32, name="out%d" % i)
            for j in range(count):
                out_of[first + j] = (out_sb, j)
            store_at[first + count - 1] = (out_sb, first, count)
            first += count

        def weight_transposes():
            w_ps["ttT"] = psum.tile([P, 8, P], BF16, name="ttT_ps", tag="acc0")
            for j in range(8):
                nc.tensor.transpose(w_ps["ttT"][:, j, :], tt_sb[:, j // 4, j % 4, :], ident_bf[:])

        def weight_transposes_out():
            nc.vector.tensor_copy(out=ttT_sb[:], in_=w_ps["ttT"][:])

        def weight_products():
            for g in range(2):
                w_ps[g] = psum.tile([P, 4, N], F32, name="w_ps%d" % g, tag="acc%d" % (1 - g))
                for t in range(4):
                    nc.tensor.matmul(
                        w_ps[g][:, t, :], lhsT=ttT_sb[:, 4 * g + t, :], rhs=core_sb[:], start=True, stop=True
                    )

        def weight_quantise():
            for g in range(2):
                nc.vector.tensor_copy(
                    out=w_grouped[:, g, :, :], in_=w_ps[g][:].rearrange("p t n -> p n t")
                )
            nc.vector.quantize_mx(
                out=w_codes[:].bitcast(FP8X4),
                scales=w_scales[:],
                in_=w_grouped[:].rearrange("p g n t -> p (g n t)"),
            )

        def sort_words(s):
            for t in step_tiles[s]:
                if is_sorted(t):
                    x_sb, j = x_of[t]
                    sorted_of[t] = work.tile(
                        [P, WORDS], F32, name="sorted%d" % t, tag="sorted%d" % (t % (2 * QUAD))
                    )
                    nc.vector.tensor_copy(
                        out=sorted_of[t][:].rearrange("p (u c i) -> p c u i", u=2, i=4),
                        in_=x_sb[:, j, :].bitcast(F32).rearrange("p (c i u) -> p c u i", u=2, i=4),
                    )

        def transposes(s):
            for t in step_tiles[s]:
                x_sb, j = x_of[t]
                words = x_sb[:, j, :].bitcast(F32)
                xt[t] = psum.tile([P, 4, P], F32, name="xt%d" % t, tag="xt%d" % (t % XT_BANKS))
                for b in range(4):
                    if t in sorted_of:
                        place = 2 * (b % 2) + b // 2
                        part = sorted_of[t][:, place * P : (place + 1) * P]
                    else:
                        first_word = 2 * P * (b // 2) + b % 2
                        part = words[:, first_word : 2 * P * (b // 2 + 1) : 2]
                    nc.tensor.transpose(xt[t][:, b, :], part, ident[:])

        def copies(s):
            grouped[s] = work.tile(
                [P, QUAD * K], BF16, name="grouped%d" % s, tag="grouped%d" % (s % 3), align_bytes=64
            )
            dst = grouped[s][:].bitcast(F32)
            for q, t in enumerate(step_tiles[s]):
                d = dst[:, q * WORDS : (q + 1) * WORDS].rearrange("p (g r u) -> p g r u", g=2, u=2)
                src = xt[t][:].rearrange("p (g u) r -> p g r u", u=2)
                if vector_copies(t):
                    nc.vector.tensor_copy(out=d, in_=src)
                else:
                    nc.scalar.copy(out=d, in_=src)

        def quantise(s):
            codes[s] = work.tile(
                [P, QUAD * K // 4], U32, name="codes%d" % s, tag="codes%d" % (s % 4), align_bytes=64
            )
            scales[s] = work.tile(
                [P, QUAD * K // 4], U8, name="scales%d" % s, tag="scales%d" % (s % 4), align_bytes=64
            )
            half = K * min(2, len(step_tiles[s]))
            for h in range((len(step_tiles[s]) + 1) // 2):
                nc.vector.quantize_mx(
                    out=codes[s][:, h * half // 4 : (h + 1) * half // 4].bitcast(FP8X4),
                    scales=scales[s][:, h * half // 4 : (h + 1) * half // 4],
                    in_=grouped[s][:, h * half : (h + 1) * half],
                )

        def acc_tag(s):
            if s >= STEPS - 2:
                return "xt%d" % ((TILES - 6 + s - (STEPS - 2)) % XT_BANKS)
            return "acc%d" % (s % 2)

        def products(s):
            acc[s] = psum.tile([P, QUAD, N], F32, name="acc%d" % s, tag=acc_tag(s))
            for q in range(len(step_tiles[s])):
                for g in range(2):
                    c0 = (2 * q + g) * P
                    nc.tensor.matmul_mx(
                        out=acc[s][:, q, :],
                        lhsT=codes[s][:, c0 : c0 + P].bitcast(FP8X4),
                        lhsT_scale=scales[s][:, c0 : c0 + P],
                        rhs=w_codes[:, g * N : (g + 1) * N].bitcast(FP8X4),
                        rhs_scale=w_scales[:, g * N : (g + 1) * N],
                        start=(g == 0),
                        stop=(g == 1),
                    )

        def results(s):
            count = len(step_tiles[s])
            out_sb, j = out_of[step_tiles[s][0]]
            if s % 3 != 2 and not STEPS - 5 < s < STEPS - 1:
                nc.vector.tensor_copy(out=out_sb[:, j : j + count, :], in_=acc[s][:, 0:count, :])
            else:
                nc.scalar.copy(out=out_sb[:, j : j + count, :], in_=acc[s][:, 0:count, :])
            last = step_tiles[s][-1]
            if last in store_at:
                tile_sb, first_tile, stored = store_at[last]
                group = first_tile // GROUP
                if stored < GROUP:
                    part = slice(first_tile % GROUP, first_tile % GROUP + stored)
                    nc.sync.dma_start(out=out_view[:, group, part, :], in_=tile_sb[:])
                else:
                    nc.sync.dma_start(
                        out=out_view[:, group : group + stored // GROUP, :, :],
                        in_=tile_sb[:].rearrange("p (s j) n -> p s j n", j=GROUP),
                    )

        for r in range(STEPS + PRODUCT_LAG + 1):
            if 0 <= r - PRODUCT_LAG - 1 < STEPS:
                results(r - PRODUCT_LAG - 1)
            if r == 1:
                weight_transposes_out()
            if 0 <= r - 1 < STEPS:
                quantise(r - 1)
            if r + 1 < STEPS:
                sort_words(r + 1)
            if r == 2:
                weight_quantise()
            if r < STEPS:
                transposes(r)
                copies(r)
            if r == 0:
                weight_transposes()
            if r == 1:
                weight_products()
            if 0 <= r - PRODUCT_LAG < STEPS:
                products(r - PRODUCT_LAG)
